import numpy as np
import ml_dtypes

BF16 = ml_dtypes.bfloat16


def bf(x):
    return np.asarray(x, np.float32).astype(BF16)


def f32(x):
    return np.asarray(x, np.float32)


def f64(x):
    return np.asarray(x).astype(np.float64)


def striped(idx):
    return np.tile(idx.reshape(-1, 16).T, (8, 1))


D, S, N, B, H, M, L1, L2 = 128, 4096, 2048, 4, 128, 512, 4096, 3072
SCALE = D ** -0.5


def soft(s):
    mx = s.max(axis=-1, keepdims=True)
    e = np.exp(s - mx)
    den = e.sum(axis=-1, keepdims=True)
    return e, den, mx + np.log(den)


def merge(oa, la, ob, lb):
    top = np.maximum(la, lb)
    l = top + np.log(np.exp(la - top) + np.exp(lb - top))
    return oa * np.exp(la - l) + ob * np.exp(lb - l), l


def setup_inputs():
    return {
        "qT": bf(3.0 * np.random.standard_normal((D, M))),
        "kpool": bf(np.random.standard_normal((D, S))),
        "v0": bf(np.random.standard_normal((N, D))),
        "k1": bf(np.random.standard_normal((B, D, L1))),
        "v1": bf(np.random.standard_normal((B, L1, D))),
        "k2": bf(np.random.standard_normal((B, D, L2))),
        "v2": bf(np.random.standard_normal((B, L2, D))),
        "offs": striped(np.random.permutation(S)[:N]),
    }


def reference(qT, kpool, v0, k1, v1, k2, v2, offs):
    idx = offs[:16].T.reshape(-1)
    s0 = SCALE * (f64(qT).T @ f64(kpool)[:, idx])
    e0, den0, lse0 = soft(s0)
    o0 = (e0 @ f64(v0)) / den0
    qb = f64(qT).T.reshape(B, H, D)
    s1 = SCALE * (qb @ f64(k1))
    e1, den1, lse1 = soft(s1)
    o1 = (e1 @ f64(v1)) / den1
    s2 = SCALE * (qb @ f64(k2))
    e2, den2, lse2 = soft(s2)
    o2 = (e2 @ f64(v2)) / den2
    o, l = merge(o0, lse0, o1.reshape(M, D), lse1.reshape(M, 1))
    o, l = merge(o, l, o2.reshape(M, D), lse2.reshape(M, 1))
    return o

@@ -1,0 +1,150 @@
+import concourse.mybir as mybir
+from concourse.masks import make_identity
+
+BF16 = mybir.dt.bfloat16
+F32 = mybir.dt.float32
+U16 = mybir.dt.uint16
+EXP = mybir.ActivationFunctionType.Exp
+ALU = mybir.AluOpType
+AXIS = mybir.AxisListType
+
+P = 128
+D, S, N, B, H, M, L1, L2 = 128, 4096, 2048, 4, 128, 512, 4096, 3072
+SCALE = D**-0.5
+UNIT = 512
+BLOCKS = UNIT // P
+STATE_UNITS = 2
+STATE = STATE_UNITS * UNIT
+STATES = (N + L1 + L2) // STATE
+SPACING = 5
+
+FLOPS = 4 * M * (N + L1 + L2) * D
+
+
+def tile_cascadeattention_b_kernel(tc, qT, kpool, v0, k1, v1, k2, v2, offs, out):
+    nc = tc.nc
+    with (
+        tc.tile_pool(name="held", bufs=1) as held,
+        tc.tile_pool(name="block", bufs=2) as block,
+        tc.tile_pool(name="small", bufs=4) as small,
+        tc.tile_pool(name="rows", bufs=4) as rows,
+        tc.tile_pool(name="columns", bufs=3) as columns,
+        tc.psum_pool(name="score_banks", bufs=4) as score_banks,
+        tc.psum_pool(name="flip_banks", bufs=2) as flip_banks,
+        tc.psum_pool(name="sum_banks", bufs=2) as sum_banks,
+    ):
+        offsets = held.tile([P, N // 16], U16, name="offsets")
+        nc.sync.dma_start(offsets[:], offs)
+        queries = held.tile([D, M], BF16, name="queries")
+        nc.sync.dma_start(queries[:], qT)
+        key_pool = held.tile([D, S], BF16, name="key_pool")
+        nc.sync.dma_start(key_pool[:], kpool)
+        identity = held.tile([P, P], BF16, name="identity")
+        make_identity(nc, identity[:])
+
+        def load_values(name, source, length):
+            values = held.tile([P, length // UNIT, BLOCKS * D], BF16, name=name)
+            nc.sync.dma_start(values[:], source.rearrange("(u p k) d -> p u (k d)", p=P, k=BLOCKS))
+            return values
+
+        def load_keys(name, source, length):
+            keys = held.tile([D, length], BF16, name=name)
+            nc.sync.dma_start(keys[:], source)
+            return keys
+
+        keys_of = {}
+        values_of = {}
+        shared_values = load_values("v0_rows", v0, N)
+        for b in range(B):
+            keys_of[(b, 0)] = key_pool
+            values_of[(b, 0)] = shared_values
+            keys_of[(b, 1)] = load_keys("k1_%d" % b, k1[b], L1)
+            values_of[(b, 1)] = load_values("v1_%d" % b, v1[b], L1)
+            keys_of[(b, 2)] = load_keys("k2_%d" % b, k2[b], L2)
+            values_of[(b, 2)] = load_values("v2_%d" % b, v2[b], L2)
+
+        shared = [(b, 0, c) for b in range(B) for c in range(N // STATE)]
+        private = [(b, level, c) for b in range(B) for level, length in ((1, L1), (2, L2)) for c in range(length // STATE)]
+        order = [
+            shared[i // SPACING] if i % SPACING == 0 else private[i - i // SPACING - 1]
+            for i in range(len(shared) + len(private))
+        ]
+        assert all(order[i][0] == i // STATES for i in range(len(order)))
+
+        for i, (b, level, c) in enumerate(order):
+            slot = i % STATES
+            if slot == 0:
+                shifts = block.tile([P, STATES], F32, name="shifts")
+                sums = block.tile([P, STATES, STATE_UNITS], F32, name="sums")
+                total = block.tile([P, D], F32, name="total")
+            keys = keys_of[(b, level)]
+            values = values_of[(b, level)]
+            units = [c * STATE_UNITS + j for j in range(STATE_UNITS)]
+
+            peaks = small.tile([P, STATE_UNITS], F32, name="peaks")
+            banks = []
+            for j, u in enumerate(units):
+                scores = score_banks.tile([P, UNIT], F32, name="scores")
+                if level == 0:
+                    moving = keys[:].indirect(offsets[:, u * UNIT // 16 : (u + 1) * UNIT // 16])
+                else:
+                    moving = keys[:, u * UNIT : (u + 1) * UNIT]
+                nc.tensor.matmul(scores[:], queries[:, b * H : (b + 1) * H], moving, start=True, stop=True)
+                nc.vector.tensor_reduce(peaks[:, j : j + 1], scores[:], axis=AXIS.X, op=ALU.max)
+                banks.append(scores)
+
+            shift = shifts[:, slot : slot + 1]
+            if slot == 0:
+                nc.vector.tensor_scalar(shift, peaks[:, 0:1], peaks[:, 1:2], -SCALE, op0=ALU.max, op1=ALU.mult)
+            else:
+                earlier = shifts[:, slot - 1 : slot]
+                own = small.tile([P, 1], F32, name="own")
+                nc.vector.tensor_scalar(own[:], peaks[:, 0:1], peaks[:, 1:2], -SCALE, op0=ALU.max, op1=ALU.mult)
+                nc.vector.tensor_tensor(shift, own[:], earlier, op=ALU.min)
+                decay = small.tile([P, 1], F32, name="decay")
+                nc.scalar.activation(decay[:], earlier, EXP, bias=shift, scale=-1.0)
+
+            flipped_bank = flip_banks.tile([P, STATE], BF16, name="flipped_bank")
+            for j in range(STATE_UNITS):
+                weights = rows.tile([P, UNIT], BF16, name="weights")
+                nc.scalar.activation(
+                    weights[:], banks[j][:], EXP, bias=shift, scale=SCALE, accum_out=sums[:, slot, j : j + 1]
+                )
+                for k in range(BLOCKS):
+                    at = (j * BLOCKS + k) * P
+                    nc.tensor.transpose(flipped_bank[:, at : at + P], weights[:, k::BLOCKS], identity[:])
+            flipped = columns.tile([P, STATE], BF16, name="flipped")
+            if i % 2 == 0:
+                nc.vector.tensor_copy(flipped[:], flipped_bank[:])
+            else:
+                nc.scalar.copy(flipped[:], flipped_bank[:])
+
+            product = sum_banks.tile([P, D], F32, name="product")
+            last = STATE_UNITS * BLOCKS - 1
+            for n in range(last + 1):
+                nc.tensor.matmul(
+                    product[:],
+                    flipped[:, n * P : (n + 1) * P],
+                    values[:, units[n // BLOCKS], (n % BLOCKS) * D : (n % BLOCKS + 1) * D],
+                    start=(n == 0),
+                    stop=(n == last),
+                )
+            if slot == 0:
+                nc.vector.tensor_copy(total[:], product[:])
+            else:
+                nc.vector.scalar_tensor_tensor(total[:], total[:], decay[:], product[:], op0=ALU.mult, op1=ALU.add)
+
+            if slot == STATES - 1:
+                rescale = small.tile([P, STATES], F32, name="rescale")
+                nc.scalar.activation(rescale[:], shifts[:], EXP, bias=shift, scale=-1.0)
+                scaled = small.tile([P, STATES, STATE_UNITS], F32, name="scaled")
+                nc.vector.tensor_tensor(
+                    scaled[:], sums[:], rescale[:].unsqueeze(2).to_broadcast([P, STATES, STATE_UNITS]), op=ALU.mult
+                )
+                denominator = small.tile([P, 1], F32, name="denominator")
+                nc.vector.tensor_reduce(denominator[:], scaled[:], axis=AXIS.XY, op=ALU.add)
+                inverse = small.tile([P, 1], F32, name="inverse")
+                nc.vector.reciprocal(inverse[:], denominator[:])
+                result = block.tile([P, D], F32, name="result")
+                nc.vector.tensor_scalar(result[:], total[:], inverse[:], None, op0=ALU.mult)
+                nc.sync.dma_start(out[b * H : (b + 1) * H, :], result[:])

@@ -15,8 +15,8 @@ UNIT = 512
 BLOCKS = UNIT // P
 STATE_UNITS = 2
 STATE = STATE_UNITS * UNIT
+SHARED_STATES = N // STATE
 STATES = (N + L1 + L2) // STATE
-SPACING = 5
 
 FLOPS = 4 * M * (N + L1 + L2) * D
 
@@ -25,126 +25,151 @@ def tile_cascadeattention_b_kernel(tc, qT, kpool, v0, k1, v1, k2, v2, offs, out)
     nc = tc.nc
     with (
         tc.tile_pool(name="held", bufs=1) as held,
-        tc.tile_pool(name="block", bufs=2) as block,
         tc.tile_pool(name="small", bufs=4) as small,
         tc.tile_pool(name="rows", bufs=4) as rows,
-        tc.tile_pool(name="columns", bufs=3) as columns,
-        tc.psum_pool(name="score_banks", bufs=4) as score_banks,
+        tc.tile_pool(name="columns", bufs=6) as columns,
+        tc.psum_pool(name="score_banks", bufs=5) as score_banks,
         tc.psum_pool(name="flip_banks", bufs=2) as flip_banks,
-        tc.psum_pool(name="sum_banks", bufs=2) as sum_banks,
+        tc.psum_pool(name="sum_banks", bufs=1) as sum_banks,
     ):
-        offsets = held.tile([P, N // 16], U16, name="offsets")
-        nc.sync.dma_start(offsets[:], offs)
-        queries = held.tile([D, M], BF16, name="queries")
-        nc.sync.dma_start(queries[:], qT)
-        key_pool = held.tile([D, S], BF16, name="key_pool")
-        nc.sync.dma_start(key_pool[:], kpool)
-        identity = held.tile([P, P], BF16, name="identity")
-        make_identity(nc, identity[:])
+        shared = [(b, 0, c, c) for b in range(B) for c in range(SHARED_STATES)]
+        private = []
+        for b in range(B):
+            stretches = [(level, c) for level, length in ((1, L1), (2, L2)) for c in range(length // STATE)]
+            private.extend((b, level, c, SHARED_STATES + n) for n, (level, c) in enumerate(stretches))
 
-        def load_values(name, source, length):
-            values = held.tile([P, length // UNIT, BLOCKS * D], BF16, name=name)
-            nc.sync.dma_start(values[:], source.rearrange("(u p k) d -> p u (k d)", p=P, k=BLOCKS))
-            return values
-
-        def load_keys(name, source, length):
-            keys = held.tile([D, length], BF16, name=name)
+        def load_keys(name, source):
+            keys = held.tile([D, source.shape[1]], BF16, name=name)
             nc.sync.dma_start(keys[:], source)
             return keys
 
+        def load_values(name, source):
+            values = held.tile([P, source.shape[0] // UNIT, BLOCKS * D], BF16, name=name)
+            nc.sync.dma_start(values[:], source.rearrange("(u p k) d -> p u (k d)", p=P, k=BLOCKS))
+            return values
+
+        queries = load_keys("queries", qT)
+        offsets = held.tile([P, N // 16], U16, name="offsets")
+        nc.sync.dma_start(offsets[:], offs)
+        key_pool = load_keys("key_pool", kpool)
+        shared_values = load_values("shared_values", v0)
         keys_of = {}
         values_of = {}
-        shared_values = load_values("v0_rows", v0, N)
         for b in range(B):
-            keys_of[(b, 0)] = key_pool
-            values_of[(b, 0)] = shared_values
-            keys_of[(b, 1)] = load_keys("k1_%d" % b, k1[b], L1)
-            values_of[(b, 1)] = load_values("v1_%d" % b, v1[b], L1)
-            keys_of[(b, 2)] = load_keys("k2_%d" % b, k2[b], L2)
-            values_of[(b, 2)] = load_values("v2_%d" % b, v2[b], L2)
+            keys_of[(b, 0)], values_of[(b, 0)] = key_pool, shared_values
+            for level, key_source, value_source in ((1, k1, v1), (2, k2, v2)):
+                keys_of[(b, level)] = load_keys("keys_%d_%d" % (b, level), key_source[b])
+                values_of[(b, level)] = load_values("values_%d_%d" % (b, level), value_source[b])
+        identity = held.tile([P, P], BF16, name="identity")
+        make_identity(nc, identity[:])
 
-        shared = [(b, 0, c) for b in range(B) for c in range(N // STATE)]
-        private = [(b, level, c) for b in range(B) for level, length in ((1, L1), (2, L2)) for c in range(length // STATE)]
-        order = [
-            shared[i // SPACING] if i % SPACING == 0 else private[i - i // SPACING - 1]
-            for i in range(len(shared) + len(private))
-        ]
-        assert all(order[i][0] == i // STATES for i in range(len(order)))
+        shifts_of = [held.tile([P, STATES], F32, name="shifts_%d" % b) for b in range(B)]
+        decays_of = [held.tile([P, STATES], F32, name="decays_%d" % b) for b in range(B)]
+        sums_of = [held.tile([P, STATES, STATE_UNITS], F32, name="sums_%d" % b) for b in range(B)]
+        total_of = [held.tile([P, D], F32, name="total_%d" % b) for b in range(B)]
+        scores_of = {}
+        flipped_of = {}
 
-        for i, (b, level, c) in enumerate(order):
-            slot = i % STATES
-            if slot == 0:
-                shifts = block.tile([P, STATES], F32, name="shifts")
-                sums = block.tile([P, STATES, STATE_UNITS], F32, name="sums")
-                total = block.tile([P, D], F32, name="total")
+        def score(state):
+            b, level, c, slot = state
             keys = keys_of[(b, level)]
-            values = values_of[(b, level)]
-            units = [c * STATE_UNITS + j for j in range(STATE_UNITS)]
-
             peaks = small.tile([P, STATE_UNITS], F32, name="peaks")
-            banks = []
-            for j, u in enumerate(units):
-                scores = score_banks.tile([P, UNIT], F32, name="scores")
+            scores_of[state] = []
+            for j in range(STATE_UNITS):
+                u = c * STATE_UNITS + j
+                if state == shared[-1] and j == STATE_UNITS - 1:
+                    scores = sum_banks.tile([P, UNIT], F32, name="scores", tag="sum_bank")
+                else:
+                    scores = score_banks.tile([P, UNIT], F32, name="scores")
                 if level == 0:
                     moving = keys[:].indirect(offsets[:, u * UNIT // 16 : (u + 1) * UNIT // 16])
                 else:
                     moving = keys[:, u * UNIT : (u + 1) * UNIT]
                 nc.tensor.matmul(scores[:], queries[:, b * H : (b + 1) * H], moving, start=True, stop=True)
                 nc.vector.tensor_reduce(peaks[:, j : j + 1], scores[:], axis=AXIS.X, op=ALU.max)
-                banks.append(scores)
-
-            shift = shifts[:, slot : slot + 1]
+                scores_of[state].append(scores)
+            shift = shifts_of[b][:, slot : slot + 1]
             if slot == 0:
                 nc.vector.tensor_scalar(shift, peaks[:, 0:1], peaks[:, 1:2], -SCALE, op0=ALU.max, op1=ALU.mult)
             else:
-                earlier = shifts[:, slot - 1 : slot]
+                earlier = shifts_of[b][:, slot - 1 : slot]
                 own = small.tile([P, 1], F32, name="own")
                 nc.vector.tensor_scalar(own[:], peaks[:, 0:1], peaks[:, 1:2], -SCALE, op0=ALU.max, op1=ALU.mult)
                 nc.vector.tensor_tensor(shift, own[:], earlier, op=ALU.min)
-                decay = small.tile([P, 1], F32, name="decay")
-                nc.scalar.activation(decay[:], earlier, EXP, bias=shift, scale=-1.0)
+                nc.scalar.activation(decays_of[b][:, slot : slot + 1], earlier, EXP, bias=shift, scale=-1.0)
 
-            flipped_bank = flip_banks.tile([P, STATE], BF16, name="flipped_bank")
+        def weigh(state):
+            b, level, c, slot = state
+            flipped_of[state] = []
             for j in range(STATE_UNITS):
                 weights = rows.tile([P, UNIT], BF16, name="weights")
                 nc.scalar.activation(
-                    weights[:], banks[j][:], EXP, bias=shift, scale=SCALE, accum_out=sums[:, slot, j : j + 1]
+                    weights[:],
+                    scores_of[state][j][:],
+                    EXP,
+                    bias=shifts_of[b][:, slot : slot + 1],
+                    scale=SCALE,
+                    accum_out=sums_of[b][:, slot, j : j + 1],
                 )
+                flipped_bank = flip_banks.tile([P, UNIT], BF16, name="flipped_bank")
                 for k in range(BLOCKS):
-                    at = (j * BLOCKS + k) * P
-                    nc.tensor.transpose(flipped_bank[:, at : at + P], weights[:, k::BLOCKS], identity[:])
-            flipped = columns.tile([P, STATE], BF16, name="flipped")
-            if i % 2 == 0:
-                nc.vector.tensor_copy(flipped[:], flipped_bank[:])
-            else:
-                nc.scalar.copy(flipped[:], flipped_bank[:])
+                    nc.tensor.transpose(flipped_bank[:, k * P : (k + 1) * P], weights[:, k::BLOCKS], identity[:])
+                if level == 0:
+                    flipped = held.tile([P, UNIT], BF16, name="flipped_%d_%d_%d" % (b, c, j))
+                else:
+                    flipped = columns.tile([P, UNIT], BF16, name="flipped")
+                if j == 0:
+                    nc.vector.tensor_copy(flipped[:], flipped_bank[:])
+                else:
+                    nc.scalar.copy(flipped[:], flipped_bank[:])
+                flipped_of[state].append(flipped)
 
-            product = sum_banks.tile([P, D], F32, name="product")
-            last = STATE_UNITS * BLOCKS - 1
-            for n in range(last + 1):
-                nc.tensor.matmul(
-                    product[:],
-                    flipped[:, n * P : (n + 1) * P],
-                    values[:, units[n // BLOCKS], (n % BLOCKS) * D : (n % BLOCKS + 1) * D],
-                    start=(n == 0),
-                    stop=(n == last),
-                )
+        def combine(state):
+            b, level, c, slot = state
+            product = sum_banks.tile([P, D], F32, name="product", tag="sum_bank")
+            for j in range(STATE_UNITS):
+                for k in range(BLOCKS):
+                    nc.tensor.matmul(
+                        product[:],
+                        flipped_of[state][j][:, k * P : (k + 1) * P],
+                        values_of[(b, level)][:, c * STATE_UNITS + j, k * D : (k + 1) * D],
+                        start=(j == 0 and k == 0),
+                        stop=(j == STATE_UNITS - 1 and k == BLOCKS - 1),
+                    )
+            total = total_of[b]
             if slot == 0:
                 nc.vector.tensor_copy(total[:], product[:])
             else:
-                nc.vector.scalar_tensor_tensor(total[:], total[:], decay[:], product[:], op0=ALU.mult, op1=ALU.add)
-
-            if slot == STATES - 1:
-                rescale = small.tile([P, STATES], F32, name="rescale")
-                nc.scalar.activation(rescale[:], shifts[:], EXP, bias=shift, scale=-1.0)
-                scaled = small.tile([P, STATES, STATE_UNITS], F32, name="scaled")
-                nc.vector.tensor_tensor(
-                    scaled[:], sums[:], rescale[:].unsqueeze(2).to_broadcast([P, STATES, STATE_UNITS]), op=ALU.mult
+                nc.vector.scalar_tensor_tensor(
+                    total[:], total[:], decays_of[b][:, slot : slot + 1], product[:], op0=ALU.mult, op1=ALU.add
                 )
-                denominator = small.tile([P, 1], F32, name="denominator")
-                nc.vector.tensor_reduce(denominator[:], scaled[:], axis=AXIS.XY, op=ALU.add)
-                inverse = small.tile([P, 1], F32, name="inverse")
-                nc.vector.reciprocal(inverse[:], denominator[:])
-                result = block.tile([P, D], F32, name="result")
-                nc.vector.tensor_scalar(result[:], total[:], inverse[:], None, op0=ALU.mult)
-                nc.sync.dma_start(out[b * H : (b + 1) * H, :], result[:])
+
+        def finish(b):
+            rescale = small.tile([P, STATES], F32, name="rescale")
+            nc.scalar.activation(rescale[:], shifts_of[b][:], EXP, bias=shifts_of[b][:, STATES - 1 : STATES], scale=-1.0)
+            scaled = small.tile([P, STATES, STATE_UNITS], F32, name="scaled")
+            nc.vector.tensor_tensor(
+                scaled[:], sums_of[b][:], rescale[:].unsqueeze(2).to_broadcast([P, STATES, STATE_UNITS]), op=ALU.mult
+            )
+            denominator = small.tile([P, 1], F32, name="denominator")
+            nc.vector.tensor_reduce(denominator[:], scaled[:], axis=AXIS.XY, op=ALU.add)
+            inverse = small.tile([P, 1], F32, name="inverse")
+            nc.vector.reciprocal(inverse[:], denominator[:])
+            result = small.tile([P, D], F32, name="result")
+            nc.vector.tensor_scalar(result[:], total_of[b][:], inverse[:], None, op0=ALU.mult)
+            nc.sync.dma_start(out[b * H : (b + 1) * H, :], result[:])
+
+        order = shared + private
+        for step in range(len(order) + 2):
+            if step < len(order):
+                score(order[step])
+            if 1 <= step <= len(order):
+                weigh(order[step - 1])
+            if step - 2 >= len(shared):
+                state = order[step - 2]
+                if state[3] == SHARED_STATES:
+                    for waiting in shared[state[0] * SHARED_STATES : (state[0] + 1) * SHARED_STATES]:
+                        combine(waiting)
+                combine(state)
+                if state[3] == STATES - 1:
+                    finish(state[0])

@@ -6,7 +6,6 @@ F32 = mybir.dt.float32
 U16 = mybir.dt.uint16
 EXP = mybir.ActivationFunctionType.Exp
 ALU = mybir.AluOpType
-AXIS = mybir.AxisListType
 
 P = 128
 D, S, N, B, H, M, L1, L2 = 128, 4096, 2048, 4, 128, 512, 4096, 3072
@@ -17,6 +16,7 @@ STATE_UNITS = 2
 STATE = STATE_UNITS * UNIT
 SHARED_STATES = N // STATE
 STATES = (N + L1 + L2) // STATE
+ROW = D + 16
 
 FLOPS = 4 * M * (N + L1 + L2) * D
 
@@ -44,8 +44,9 @@ def tile_cascadeattention_b_kernel(tc, qT, kpool, v0, k1, v1, k2, v2, offs, out)
             return keys
 
         def load_values(name, source):
-            values = held.tile([P, source.shape[0] // UNIT, BLOCKS * D], BF16, name=name)
-            nc.sync.dma_start(values[:], source.rearrange("(u p k) d -> p u (k d)", p=P, k=BLOCKS))
+            values = held.tile([P, source.shape[0] // P, ROW], BF16, name=name)
+            nc.gpsimd.memset(values[:, :, D:ROW], 1.0)
+            nc.sync.dma_start(values[:, :, 0:D], source.rearrange("(r p) d -> p r d", p=P))
             return values
 
         queries = load_keys("queries", qT)
@@ -63,17 +64,19 @@ def tile_cascadeattention_b_kernel(tc, qT, kpool, v0, k1, v1, k2, v2, offs, out)
         identity = held.tile([P, P], BF16, name="identity")
         make_identity(nc, identity[:])
 
-        shifts_of = [held.tile([P, STATES], F32, name="shifts_%d" % b) for b in range(B)]
+        shifts_of = [held.tile([P, STATES * STATE_UNITS], F32, name="shifts_%d" % b) for b in range(B)]
         decays_of = [held.tile([P, STATES], F32, name="decays_%d" % b) for b in range(B)]
-        sums_of = [held.tile([P, STATES, STATE_UNITS], F32, name="sums_%d" % b) for b in range(B)]
-        total_of = [held.tile([P, D], F32, name="total_%d" % b) for b in range(B)]
+        total_of = [held.tile([P, D + 1], F32, name="total_%d" % b) for b in range(B)]
         scores_of = {}
         flipped_of = {}
+
+        def shift_of(b, slot):
+            last_unit = (slot + 1) * STATE_UNITS - 1
+            return shifts_of[b][:, last_unit : last_unit + 1]
 
         def score(state):
             b, level, c, slot = state
             keys = keys_of[(b, level)]
-            peaks = small.tile([P, STATE_UNITS], F32, name="peaks")
             scores_of[state] = []
             for j in range(STATE_UNITS):
                 u = c * STATE_UNITS + j
@@ -86,17 +89,22 @@ def tile_cascadeattention_b_kernel(tc, qT, kpool, v0, k1, v1, k2, v2, offs, out)
                 else:
                     moving = keys[:, u * UNIT : (u + 1) * UNIT]
                 nc.tensor.matmul(scores[:], queries[:, b * H : (b + 1) * H], moving, start=True, stop=True)
-                nc.vector.tensor_reduce(peaks[:, j : j + 1], scores[:], axis=AXIS.X, op=ALU.max)
+                n = slot * STATE_UNITS + j
+                scaled = rows.tile([P, UNIT], BF16, name="scaled")
+                nc.vector.tensor_scalar(
+                    scaled[:],
+                    scores[:],
+                    -SCALE,
+                    shifts_of[b][:, n - 1 : n] if n > 0 else None,
+                    op0=ALU.mult,
+                    op1=ALU.min,
+                    accum_out=shifts_of[b][:, n : n + 1],
+                )
                 scores_of[state].append(scores)
-            shift = shifts_of[b][:, slot : slot + 1]
-            if slot == 0:
-                nc.vector.tensor_scalar(shift, peaks[:, 0:1], peaks[:, 1:2], -SCALE, op0=ALU.max, op1=ALU.mult)
-            else:
-                earlier = shifts_of[b][:, slot - 1 : slot]
-                own = small.tile([P, 1], F32, name="own")
-                nc.vector.tensor_scalar(own[:], peaks[:, 0:1], peaks[:, 1:2], -SCALE, op0=ALU.max, op1=ALU.mult)
-                nc.vector.tensor_tensor(shift, own[:], earlier, op=ALU.min)
-                nc.scalar.activation(decays_of[b][:, slot : slot + 1], earlier, EXP, bias=shift, scale=-1.0)
+            if slot > 0:
+                nc.scalar.activation(
+                    decays_of[b][:, slot : slot + 1], shift_of(b, slot - 1), EXP, bias=shift_of(b, slot), scale=-1.0
+                )
 
         def weigh(state):
             b, level, c, slot = state
@@ -104,35 +112,30 @@ def tile_cascadeattention_b_kernel(tc, qT, kpool, v0, k1, v1, k2, v2, offs, out)
             for j in range(STATE_UNITS):
                 weights = rows.tile([P, UNIT], BF16, name="weights")
                 nc.scalar.activation(
-                    weights[:],
-                    scores_of[state][j][:],
-                    EXP,
-                    bias=shifts_of[b][:, slot : slot + 1],
-                    scale=SCALE,
-                    accum_out=sums_of[b][:, slot, j : j + 1],
+                    weights[:], scores_of[state][j][:], EXP, bias=shift_of(b, slot), scale=SCALE
                 )
                 flipped_bank = flip_banks.tile([P, UNIT], BF16, name="flipped_bank")
                 for k in range(BLOCKS):
-                    nc.tensor.transpose(flipped_bank[:, k * P : (k + 1) * P], weights[:, k::BLOCKS], identity[:])
+                    nc.tensor.transpose(flipped_bank[:, k * P : (k + 1) * P], weights[:, k * P : (k + 1) * P], identity[:])
                 if level == 0:
                     flipped = held.tile([P, UNIT], BF16, name="flipped_%d_%d_%d" % (b, c, j))
                 else:
                     flipped = columns.tile([P, UNIT], BF16, name="flipped")
                 if j == 0:
-                    nc.vector.tensor_copy(flipped[:], flipped_bank[:])
-                else:
                     nc.scalar.copy(flipped[:], flipped_bank[:])
+                else:
+                    nc.vector.tensor_copy(flipped[:], flipped_bank[:])
                 flipped_of[state].append(flipped)
 
         def combine(state):
             b, level, c, slot = state
-            product = sum_banks.tile([P, D], F32, name="product", tag="sum_bank")
+            product = sum_banks.tile([P, D + 1], F32, name="product", tag="sum_bank")
             for j in range(STATE_UNITS):
                 for k in range(BLOCKS):
                     nc.tensor.matmul(
                         product[:],
                         flipped_of[state][j][:, k * P : (k + 1) * P],
-                        values_of[(b, level)][:, c * STATE_UNITS + j, k * D : (k + 1) * D],
+                        values_of[(b, level)][:, (c * STATE_UNITS + j) * BLOCKS + k, 0 : D + 1],
                         start=(j == 0 and k == 0),
                         stop=(j == STATE_UNITS - 1 and k == BLOCKS - 1),
                     )
@@ -145,18 +148,10 @@ def tile_cascadeattention_b_kernel(tc, qT, kpool, v0, k1, v1, k2, v2, offs, out)
                 )
 
         def finish(b):
-            rescale = small.tile([P, STATES], F32, name="rescale")
-            nc.scalar.activation(rescale[:], shifts_of[b][:], EXP, bias=shifts_of[b][:, STATES - 1 : STATES], scale=-1.0)
-            scaled = small.tile([P, STATES, STATE_UNITS], F32, name="scaled")
-            nc.vector.tensor_tensor(
-                scaled[:], sums_of[b][:], rescale[:].unsqueeze(2).to_broadcast([P, STATES, STATE_UNITS]), op=ALU.mult
-            )
-            denominator = small.tile([P, 1], F32, name="denominator")
-            nc.vector.tensor_reduce(denominator[:], scaled[:], axis=AXIS.XY, op=ALU.add)
             inverse = small.tile([P, 1], F32, name="inverse")
-            nc.vector.reciprocal(inverse[:], denominator[:])
+            nc.vector.reciprocal(inverse[:], total_of[b][:, D : D + 1])
             result = small.tile([P, D], F32, name="result")
-            nc.vector.tensor_scalar(result[:], total_of[b][:], inverse[:], None, op0=ALU.mult)
+            nc.vector.tensor_scalar(result[:], total_of[b][:, 0:D], inverse[:], None, op0=ALU.mult)
             nc.sync.dma_start(out[b * H : (b + 1) * H, :], result[:])
 
         order = shared + private

@@ -6,6 +6,7 @@ F32 = mybir.dt.float32
 U16 = mybir.dt.uint16
 EXP = mybir.ActivationFunctionType.Exp
 ALU = mybir.AluOpType
+AXIS = mybir.AxisListType
 
 P = 128
 D, S, N, B, H, M, L1, L2 = 128, 4096, 2048, 4, 128, 512, 4096, 3072
@@ -14,8 +15,8 @@ UNIT = 512
 BLOCKS = UNIT // P
 STATE_UNITS = 2
 STATE = STATE_UNITS * UNIT
-SHARED_STATES = N // STATE
 STATES = (N + L1 + L2) // STATE
+EARLY = 2
 ROW = D + 16
 
 FLOPS = 4 * M * (N + L1 + L2) * D
@@ -26,22 +27,36 @@ def tile_cascadeattention_b_kernel(tc, qT, kpool, v0, k1, v1, k2, v2, offs, out)
     with (
         tc.tile_pool(name="held", bufs=1) as held,
         tc.tile_pool(name="small", bufs=4) as small,
+        tc.tile_pool(name="ahead", bufs=8) as ahead,
         tc.tile_pool(name="rows", bufs=4) as rows,
-        tc.tile_pool(name="columns", bufs=6) as columns,
-        tc.psum_pool(name="score_banks", bufs=5) as score_banks,
-        tc.psum_pool(name="flip_banks", bufs=2) as flip_banks,
-        tc.psum_pool(name="sum_banks", bufs=1) as sum_banks,
+        tc.tile_pool(name="columns", bufs=8) as columns,
+        tc.psum_pool(name="score_banks", bufs=3) as score_banks,
+        tc.psum_pool(name="flip_banks", bufs=3) as flip_banks,
+        tc.psum_pool(name="sum_banks", bufs=2) as sum_banks,
     ):
-        shared = [(b, 0, c, c) for b in range(B) for c in range(SHARED_STATES)]
-        private = []
-        for b in range(B):
-            stretches = [(level, c) for level, length in ((1, L1), (2, L2)) for c in range(length // STATE)]
-            private.extend((b, level, c, SHARED_STATES + n) for n, (level, c) in enumerate(stretches))
+        shared = [(b, 0, c) for b in range(B) for c in range(N // STATE)]
+        private = [
+            (b, level, c) for b in range(B) for level, length in ((1, L1), (2, L2)) for c in range(length // STATE)
+        ]
+        waiting = private[:EARLY] + shared
+        order = waiting + private[EARLY:]
+        slot_of = {}
+        for state in order:
+            slot_of[state] = len([other for other in slot_of if other[0] == state[0]])
 
-        def load_keys(name, source):
-            keys = held.tile([D, source.shape[1]], BF16, name=name)
-            nc.sync.dma_start(keys[:], source)
-            return keys
+        key_sources = {1: k1, 2: k2}
+        value_sources = {1: v1, 2: v2}
+        keys_of = {}
+        values_of = {}
+
+        def load_keys(state):
+            b, level, c = state
+            source = key_sources[level][b]
+            if (b, level) not in keys_of:
+                keys_of[(b, level)] = held.tile([D, source.shape[1]], BF16, name="keys_%d_%d" % (b, level))
+            nc.sync.dma_start(
+                keys_of[(b, level)][:, c * STATE : (c + 1) * STATE], source[:, c * STATE : (c + 1) * STATE]
+            )
 
         def load_values(name, source):
             values = held.tile([P, source.shape[0] // P, ROW], BF16, name=name)
@@ -49,86 +64,90 @@ def tile_cascadeattention_b_kernel(tc, qT, kpool, v0, k1, v1, k2, v2, offs, out)
             nc.sync.dma_start(values[:, :, 0:D], source.rearrange("(r p) d -> p r d", p=P))
             return values
 
-        queries = load_keys("queries", qT)
+        queries = held.tile([D, M], BF16, name="queries")
+        nc.sync.dma_start(queries[:], qT)
+        for state in private[:EARLY]:
+            load_keys(state)
         offsets = held.tile([P, N // 16], U16, name="offsets")
         nc.sync.dma_start(offsets[:], offs)
-        key_pool = load_keys("key_pool", kpool)
+        key_pool = held.tile([D, S], BF16, name="key_pool")
+        nc.sync.dma_start(key_pool[:], kpool)
         shared_values = load_values("shared_values", v0)
-        keys_of = {}
-        values_of = {}
         for b in range(B):
             keys_of[(b, 0)], values_of[(b, 0)] = key_pool, shared_values
-            for level, key_source, value_source in ((1, k1, v1), (2, k2, v2)):
-                keys_of[(b, level)] = load_keys("keys_%d_%d" % (b, level), key_source[b])
-                values_of[(b, level)] = load_values("values_%d_%d" % (b, level), value_source[b])
+        for state in private[EARLY:]:
+            load_keys(state)
+            b, level, c = state
+            if (c + 1) * STATE == keys_of[(b, level)].shape[1]:
+                values_of[(b, level)] = load_values("values_%d_%d" % (b, level), value_sources[level][b])
         identity = held.tile([P, P], BF16, name="identity")
         make_identity(nc, identity[:])
 
-        shifts_of = [held.tile([P, STATES * STATE_UNITS], F32, name="shifts_%d" % b) for b in range(B)]
+        lowest_of = [held.tile([P, STATES * STATE_UNITS], F32, name="lowest_%d" % b) for b in range(B)]
+        shifts_of = [held.tile([P, STATES], F32, name="shifts_%d" % b) for b in range(B)]
         decays_of = [held.tile([P, STATES], F32, name="decays_%d" % b) for b in range(B)]
         total_of = [held.tile([P, D + 1], F32, name="total_%d" % b) for b in range(B)]
-        scores_of = {}
+        scaled_of = {}
         flipped_of = {}
 
-        def shift_of(b, slot):
-            last_unit = (slot + 1) * STATE_UNITS - 1
-            return shifts_of[b][:, last_unit : last_unit + 1]
-
         def score(state):
-            b, level, c, slot = state
-            keys = keys_of[(b, level)]
-            scores_of[state] = []
+            b, level, c = state
+            slot = slot_of[state]
+            scaled_of[state] = []
             for j in range(STATE_UNITS):
                 u = c * STATE_UNITS + j
-                if state == shared[-1] and j == STATE_UNITS - 1:
+                if state == shared[-1]:
                     scores = sum_banks.tile([P, UNIT], F32, name="scores", tag="sum_bank")
                 else:
                     scores = score_banks.tile([P, UNIT], F32, name="scores")
                 if level == 0:
-                    moving = keys[:].indirect(offsets[:, u * UNIT // 16 : (u + 1) * UNIT // 16])
+                    moving = key_pool[:].indirect(offsets[:, u * UNIT // 16 : (u + 1) * UNIT // 16])
                 else:
-                    moving = keys[:, u * UNIT : (u + 1) * UNIT]
+                    moving = keys_of[(b, level)][:, u * UNIT : (u + 1) * UNIT]
                 nc.tensor.matmul(scores[:], queries[:, b * H : (b + 1) * H], moving, start=True, stop=True)
                 n = slot * STATE_UNITS + j
-                scaled = rows.tile([P, UNIT], BF16, name="scaled")
+                scaled = ahead.tile([P, UNIT], F32, name="scaled")
                 nc.vector.tensor_scalar(
-                    scaled[:],
-                    scores[:],
-                    -SCALE,
-                    shifts_of[b][:, n - 1 : n] if n > 0 else None,
-                    op0=ALU.mult,
-                    op1=ALU.min,
-                    accum_out=shifts_of[b][:, n : n + 1],
+                    scaled[:], scores[:], -SCALE, None, op0=ALU.mult, op1=ALU.min, accum_out=lowest_of[b][:, n : n + 1]
                 )
-                scores_of[state].append(scores)
+                scaled_of[state].append(scaled)
+            nc.vector.tensor_reduce(
+                shifts_of[b][:, slot : slot + 1], lowest_of[b][:, 0 : (slot + 1) * STATE_UNITS], axis=AXIS.X, op=ALU.min
+            )
             if slot > 0:
                 nc.scalar.activation(
-                    decays_of[b][:, slot : slot + 1], shift_of(b, slot - 1), EXP, bias=shift_of(b, slot), scale=-1.0
+                    decays_of[b][:, slot : slot + 1],
+                    shifts_of[b][:, slot - 1 : slot],
+                    EXP,
+                    bias=shifts_of[b][:, slot : slot + 1],
+                    scale=-1.0,
                 )
 
         def weigh(state):
-            b, level, c, slot = state
+            b, level, c = state
+            slot = slot_of[state]
             flipped_of[state] = []
             for j in range(STATE_UNITS):
                 weights = rows.tile([P, UNIT], BF16, name="weights")
                 nc.scalar.activation(
-                    weights[:], scores_of[state][j][:], EXP, bias=shift_of(b, slot), scale=SCALE
+                    weights[:], scaled_of[state][j][:], EXP, bias=shifts_of[b][:, slot : slot + 1], scale=-1.0
                 )
                 flipped_bank = flip_banks.tile([P, UNIT], BF16, name="flipped_bank")
                 for k in range(BLOCKS):
                     nc.tensor.transpose(flipped_bank[:, k * P : (k + 1) * P], weights[:, k * P : (k + 1) * P], identity[:])
-                if level == 0:
-                    flipped = held.tile([P, UNIT], BF16, name="flipped_%d_%d_%d" % (b, c, j))
+                if state in waiting:
+                    flipped = held.tile([P, UNIT], BF16, name="flipped_%d_%d_%d_%d" % (b, level, c, j))
                 else:
                     flipped = columns.tile([P, UNIT], BF16, name="flipped")
-                if j == 0:
+                if j == 0 and level > 0:
                     nc.scalar.copy(flipped[:], flipped_bank[:])
                 else:
                     nc.vector.tensor_copy(flipped[:], flipped_bank[:])
                 flipped_of[state].append(flipped)
 
         def combine(state):
-            b, level, c, slot = state
+            b, level, c = state
+            slot = slot_of[state]
             product = sum_banks.tile([P, D + 1], F32, name="product", tag="sum_bank")
             for j in range(STATE_UNITS):
                 for k in range(BLOCKS):
@@ -154,17 +173,17 @@ def tile_cascadeattention_b_kernel(tc, qT, kpool, v0, k1, v1, k2, v2, offs, out)
             nc.vector.tensor_scalar(result[:], total_of[b][:, 0:D], inverse[:], None, op0=ALU.mult)
             nc.sync.dma_start(out[b * H : (b + 1) * H, :], result[:])
 
-        order = shared + private
-        for step in range(len(order) + 2):
+        for step in range(len(order) + 3):
             if step < len(order):
                 score(order[step])
-            if 1 <= step <= len(order):
-                weigh(order[step - 1])
-            if step - 2 >= len(shared):
-                state = order[step - 2]
-                if state[3] == SHARED_STATES:
-                    for waiting in shared[state[0] * SHARED_STATES : (state[0] + 1) * SHARED_STATES]:
-                        combine(waiting)
+            if 2 <= step < len(order) + 2:
+                weigh(order[step - 2])
+            if step - 3 >= len(waiting):
+                state = order[step - 3]
+                earlier = [other for other in waiting if other[0] == state[0]]
+                if slot_of[state] == len(earlier):
+                    for other in earlier:
+                        combine(other)
                 combine(state)
-                if state[3] == STATES - 1:
+                if slot_of[state] == STATES - 1:
                     finish(state[0])

@@ -16,7 +16,6 @@ BLOCKS = UNIT // P
 STATE_UNITS = 2
 STATE = STATE_UNITS * UNIT
 STATES = (N + L1 + L2) // STATE
-EARLY = 2
 ROW = D + 16
 
 FLOPS = 4 * M * (N + L1 + L2) * D
@@ -38,25 +37,15 @@ def tile_cascadeattention_b_kernel(tc, qT, kpool, v0, k1, v1, k2, v2, offs, out)
         private = [
             (b, level, c) for b in range(B) for level, length in ((1, L1), (2, L2)) for c in range(length // STATE)
         ]
-        waiting = private[:EARLY] + shared
-        order = waiting + private[EARLY:]
+        order = shared + private
         slot_of = {}
         for state in order:
             slot_of[state] = len([other for other in slot_of if other[0] == state[0]])
 
-        key_sources = {1: k1, 2: k2}
-        value_sources = {1: v1, 2: v2}
-        keys_of = {}
-        values_of = {}
-
-        def load_keys(state):
-            b, level, c = state
-            source = key_sources[level][b]
-            if (b, level) not in keys_of:
-                keys_of[(b, level)] = held.tile([D, source.shape[1]], BF16, name="keys_%d_%d" % (b, level))
-            nc.sync.dma_start(
-                keys_of[(b, level)][:, c * STATE : (c + 1) * STATE], source[:, c * STATE : (c + 1) * STATE]
-            )
+        def load_keys(name, source):
+            keys = held.tile([D, source.shape[1]], BF16, name=name)
+            nc.sync.dma_start(keys[:], source)
+            return keys
 
         def load_values(name, source):
             values = held.tile([P, source.shape[0] // P, ROW], BF16, name=name)
@@ -64,22 +53,18 @@ def tile_cascadeattention_b_kernel(tc, qT, kpool, v0, k1, v1, k2, v2, offs, out)
             nc.sync.dma_start(values[:, :, 0:D], source.rearrange("(r p) d -> p r d", p=P))
             return values
 
-        queries = held.tile([D, M], BF16, name="queries")
-        nc.sync.dma_start(queries[:], qT)
-        for state in private[:EARLY]:
-            load_keys(state)
+        queries = load_keys("queries", qT)
         offsets = held.tile([P, N // 16], U16, name="offsets")
         nc.sync.dma_start(offsets[:], offs)
-        key_pool = held.tile([D, S], BF16, name="key_pool")
-        nc.sync.dma_start(key_pool[:], kpool)
+        key_pool = load_keys("key_pool", kpool)
         shared_values = load_values("shared_values", v0)
+        keys_of = {}
+        values_of = {}
         for b in range(B):
-            keys_of[(b, 0)], values_of[(b, 0)] = key_pool, shared_values
-        for state in private[EARLY:]:
-            load_keys(state)
-            b, level, c = state
-            if (c + 1) * STATE == keys_of[(b, level)].shape[1]:
-                values_of[(b, level)] = load_values("values_%d_%d" % (b, level), value_sources[level][b])
+            values_of[(b, 0)] = shared_values
+            for level, key_source, value_source in ((1, k1, v1), (2, k2, v2)):
+                keys_of[(b, level)] = load_keys("keys_%d_%d" % (b, level), key_source[b])
+                values_of[(b, level)] = load_values("values_%d_%d" % (b, level), value_source[b])
         identity = held.tile([P, P], BF16, name="identity")
         make_identity(nc, identity[:])
 
@@ -135,8 +120,8 @@ def tile_cascadeattention_b_kernel(tc, qT, kpool, v0, k1, v1, k2, v2, offs, out)
                 flipped_bank = flip_banks.tile([P, UNIT], BF16, name="flipped_bank")
                 for k in range(BLOCKS):
                     nc.tensor.transpose(flipped_bank[:, k * P : (k + 1) * P], weights[:, k * P : (k + 1) * P], identity[:])
-                if state in waiting:
-                    flipped = held.tile([P, UNIT], BF16, name="flipped_%d_%d_%d_%d" % (b, level, c, j))
+                if level == 0:
+                    flipped = held.tile([P, UNIT], BF16, name="flipped_%d_%d_%d" % (b, c, j))
                 else:
                     flipped = columns.tile([P, UNIT], BF16, name="flipped")
                 if j == 0 and level > 0:
@@ -178,11 +163,11 @@ def tile_cascadeattention_b_kernel(tc, qT, kpool, v0, k1, v1, k2, v2, offs, out)
                 score(order[step])
             if 2 <= step < len(order) + 2:
                 weigh(order[step - 2])
-            if step - 3 >= len(waiting):
+            if step - 3 >= len(shared):
                 state = order[step - 3]
-                earlier = [other for other in waiting if other[0] == state[0]]
-                if slot_of[state] == len(earlier):
-                    for other in earlier:
+                waiting = [other for other in shared if other[0] == state[0]]
+                if slot_of[state] == len(waiting):
+                    for other in waiting:
                         combine(other)
                 combine(state)
                 if slot_of[state] == STATES - 1:

@@ -12,9 +12,11 @@ P = 128
 D, S, N, B, H, M, L1, L2 = 128, 4096, 2048, 4, 128, 512, 4096, 3072
 SCALE = D**-0.5
 UNIT = 512
-BLOCKS = UNIT // P
+PAIR = 2
+GROUP = PAIR * P
 STATE_UNITS = 2
 STATE = STATE_UNITS * UNIT
+GROUPS = STATE // GROUP
 STATES = (N + L1 + L2) // STATE
 ROW = D + 16
 
@@ -28,7 +30,7 @@ def tile_cascadeattention_b_kernel(tc, qT, kpool, v0, k1, v1, k2, v2, offs, out)
         tc.tile_pool(name="small", bufs=4) as small,
         tc.tile_pool(name="ahead", bufs=8) as ahead,
         tc.tile_pool(name="rows", bufs=4) as rows,
-        tc.tile_pool(name="columns", bufs=8) as columns,
+        tc.tile_pool(name="columns", bufs=4) as columns,
         tc.psum_pool(name="score_banks", bufs=3) as score_banks,
         tc.psum_pool(name="flip_banks", bufs=3) as flip_banks,
         tc.psum_pool(name="sum_banks", bufs=2) as sum_banks,
@@ -48,9 +50,11 @@ def tile_cascadeattention_b_kernel(tc, qT, kpool, v0, k1, v1, k2, v2, offs, out)
             return keys
 
         def load_values(name, source):
-            values = held.tile([P, source.shape[0] // P, ROW], BF16, name=name)
-            nc.gpsimd.memset(values[:, :, D:ROW], 1.0)
-            nc.sync.dma_start(values[:, :, 0:D], source.rearrange("(r p) d -> p r d", p=P))
+            values = held.tile([P, source.shape[0] // GROUP, PAIR, ROW], BF16, name=name)
+            nc.gpsimd.memset(values[:, :, :, D:ROW], 1.0)
+            by_parity = source.rearrange("(g p r) d -> p g r d", p=P, r=PAIR)
+            for r in range(PAIR):
+                nc.sync.dma_start(values[:, :, r, 0:D], by_parity[:, :, r, :])
             return values
 
         queries = load_keys("queries", qT)
@@ -65,7 +69,7 @@ def tile_cascadeattention_b_kernel(tc, qT, kpool, v0, k1, v1, k2, v2, offs, out)
             for level, key_source, value_source in ((1, k1, v1), (2, k2, v2)):
                 keys_of[(b, level)] = load_keys("keys_%d_%d" % (b, level), key_source[b])
                 values_of[(b, level)] = load_values("values_%d_%d" % (b, level), value_source[b])
-        identity = held.tile([P, P], BF16, name="identity")
+        identity = held.tile([P, P], F32, name="identity")
         make_identity(nc, identity[:])
 
         lowest_of = [held.tile([P, STATES * STATE_UNITS], F32, name="lowest_%d" % b) for b in range(B)]
@@ -111,37 +115,42 @@ def tile_cascadeattention_b_kernel(tc, qT, kpool, v0, k1, v1, k2, v2, offs, out)
         def weigh(state):
             b, level, c = state
             slot = slot_of[state]
-            flipped_of[state] = []
+            weights = rows.tile([P, STATE], BF16, name="weights")
             for j in range(STATE_UNITS):
-                weights = rows.tile([P, UNIT], BF16, name="weights")
                 nc.scalar.activation(
-                    weights[:], scaled_of[state][j][:], EXP, bias=shifts_of[b][:, slot : slot + 1], scale=-1.0
+                    weights[:, j * UNIT : (j + 1) * UNIT],
+                    scaled_of[state][j][:],
+                    EXP,
+                    bias=shifts_of[b][:, slot : slot + 1],
+                    scale=-1.0,
                 )
-                flipped_bank = flip_banks.tile([P, UNIT], BF16, name="flipped_bank")
-                for k in range(BLOCKS):
-                    nc.tensor.transpose(flipped_bank[:, k * P : (k + 1) * P], weights[:, k * P : (k + 1) * P], identity[:])
-                if level == 0:
-                    flipped = held.tile([P, UNIT], BF16, name="flipped_%d_%d_%d" % (b, c, j))
-                else:
-                    flipped = columns.tile([P, UNIT], BF16, name="flipped")
-                if j == 0 and level > 0:
-                    nc.scalar.copy(flipped[:], flipped_bank[:])
-                else:
-                    nc.vector.tensor_copy(flipped[:], flipped_bank[:])
-                flipped_of[state].append(flipped)
+            words = weights[:].bitcast(F32)
+            flipped_bank = flip_banks.tile([P, GROUPS * P], F32, name="flipped_bank")
+            for k in range(GROUPS):
+                nc.tensor.transpose(flipped_bank[:, k * P : (k + 1) * P], words[:, k * P : (k + 1) * P], identity[:])
+            if level == 0:
+                flipped = held.tile([P, STATE], BF16, name="flipped_%d_%d" % (b, c))
+            else:
+                flipped = columns.tile([P, STATE], BF16, name="flipped")
+            if level > 0 and slot % 2 == 0:
+                nc.scalar.copy(flipped[:], flipped_bank[:].bitcast(BF16))
+            else:
+                nc.vector.tensor_copy(flipped[:], flipped_bank[:].bitcast(BF16))
+            flipped_of[state] = flipped
 
         def combine(state):
             b, level, c = state
             slot = slot_of[state]
             product = sum_banks.tile([P, D + 1], F32, name="product", tag="sum_bank")
-            for j in range(STATE_UNITS):
-                for k in range(BLOCKS):
+            halves = flipped_of[state]
+            for k in range(GROUPS):
+                for r in range(PAIR):
                     nc.tensor.matmul(
                         product[:],
-                        flipped_of[state][j][:, k * P : (k + 1) * P],
-                        values_of[(b, level)][:, (c * STATE_UNITS + j) * BLOCKS + k, 0 : D + 1],
-                        start=(j == 0 and k == 0),
-                        stop=(j == STATE_UNITS - 1 and k == BLOCKS - 1),
+                        halves[:, k * GROUP + r : (k + 1) * GROUP : PAIR],
+                        values_of[(b, level)][:, c * GROUPS + k, r, 0 : D + 1],
+                        start=(k == 0 and r == 0),
+                        stop=(k == GROUPS - 1 and r == PAIR - 1),
                     )
             total = total_of[b]
             if slot == 0:

@@ -9,16 +9,22 @@ ALU = mybir.AluOpType
 AXIS = mybir.AxisListType
 
 P = 128
-D, S, N, B, H, M, L1, L2 = 128, 4096, 2048, 4, 128, 512, 4096, 3072
+D, N, B, H, M, L1, L2 = 128, 2048, 4, 128, 512, 4096, 3072
 SCALE = D**-0.5
 UNIT = 512
+PIECE_UNITS = 2
+PIECE = PIECE_UNITS * UNIT
+STATE_PIECES = 2
+LENGTH = (N, L1, L2)
+FIRST_UNIT = (0, N // UNIT, (N + L1) // UNIT)
+UNITS = (N + L1 + L2) // UNIT
 PAIR = 2
 GROUP = PAIR * P
-STATE_UNITS = 2
-STATE = STATE_UNITS * UNIT
-GROUPS = STATE // GROUP
-STATES = (N + L1 + L2) // STATE
+GROUPS = PIECE // GROUP
 ROW = D + 16
+
+WEIGH_LAG = 4
+COMBINE_LAG = 7
 
 FLOPS = 4 * M * (N + L1 + L2) * D
 
@@ -28,21 +34,33 @@ def tile_cascadeattention_b_kernel(tc, qT, kpool, v0, k1, v1, k2, v2, offs, out)
     with (
         tc.tile_pool(name="held", bufs=1) as held,
         tc.tile_pool(name="small", bufs=4) as small,
-        tc.tile_pool(name="ahead", bufs=8) as ahead,
+        tc.tile_pool(name="ahead", bufs=10) as ahead,
         tc.tile_pool(name="rows", bufs=4) as rows,
-        tc.tile_pool(name="columns", bufs=4) as columns,
+        tc.tile_pool(name="columns", bufs=12) as columns,
         tc.psum_pool(name="score_banks", bufs=3) as score_banks,
         tc.psum_pool(name="flip_banks", bufs=3) as flip_banks,
         tc.psum_pool(name="sum_banks", bufs=2) as sum_banks,
     ):
-        shared = [(b, 0, c) for b in range(B) for c in range(N // STATE)]
-        private = [
-            (b, level, c) for b in range(B) for level, length in ((1, L1), (2, L2)) for c in range(length // STATE)
-        ]
+        shared = [(b, 0, c) for b in range(B) for c in range(LENGTH[0] // PIECE)]
+        private = [(b, level, c) for b in range(B) for level in (1, 2) for c in range(LENGTH[level] // PIECE)]
         order = shared + private
+
+        def state_of(piece):
+            b, level, c = piece
+            return (b, level, c // STATE_PIECES)
+
+        def opens_state(piece):
+            return piece[2] % STATE_PIECES == 0
+
+        def closes_state(piece):
+            b, level, c = piece
+            return c % STATE_PIECES == STATE_PIECES - 1 or c == LENGTH[level] // PIECE - 1
+
         slot_of = {}
-        for state in order:
-            slot_of[state] = len([other for other in slot_of if other[0] == state[0]])
+        for piece in order:
+            if opens_state(piece):
+                slot_of[state_of(piece)] = len([other for other in slot_of if other[0] == piece[0]])
+        states = len([state for state in slot_of if state[0] == 0])
 
         def load_keys(name, source):
             keys = held.tile([D, source.shape[1]], BF16, name=name)
@@ -72,20 +90,20 @@ def tile_cascadeattention_b_kernel(tc, qT, kpool, v0, k1, v1, k2, v2, offs, out)
         identity = held.tile([P, P], F32, name="identity")
         make_identity(nc, identity[:])
 
-        lowest_of = [held.tile([P, STATES * STATE_UNITS], F32, name="lowest_%d" % b) for b in range(B)]
-        shifts_of = [held.tile([P, STATES], F32, name="shifts_%d" % b) for b in range(B)]
-        decays_of = [held.tile([P, STATES], F32, name="decays_%d" % b) for b in range(B)]
+        lowest_of = [held.tile([P, UNITS], F32, name="lowest_%d" % b) for b in range(B)]
+        shifts_of = [held.tile([P, states], F32, name="shifts_%d" % b) for b in range(B)]
+        decays_of = [held.tile([P, states], F32, name="decays_%d" % b) for b in range(B)]
         total_of = [held.tile([P, D + 1], F32, name="total_%d" % b) for b in range(B)]
         scaled_of = {}
         flipped_of = {}
+        product_of = {}
 
-        def score(state):
-            b, level, c = state
-            slot = slot_of[state]
-            scaled_of[state] = []
-            for j in range(STATE_UNITS):
-                u = c * STATE_UNITS + j
-                if state == shared[-1]:
+        def score(piece):
+            b, level, c = piece
+            scaled = ahead.tile([P, PIECE], F32, name="scaled")
+            for j in range(PIECE_UNITS):
+                u = c * PIECE_UNITS + j
+                if piece == shared[-1]:
                     scores = sum_banks.tile([P, UNIT], F32, name="scores", tag="sum_bank")
                 else:
                     scores = score_banks.tile([P, UNIT], F32, name="scores")
@@ -94,15 +112,25 @@ def tile_cascadeattention_b_kernel(tc, qT, kpool, v0, k1, v1, k2, v2, offs, out)
                 else:
                     moving = keys_of[(b, level)][:, u * UNIT : (u + 1) * UNIT]
                 nc.tensor.matmul(scores[:], queries[:, b * H : (b + 1) * H], moving, start=True, stop=True)
-                n = slot * STATE_UNITS + j
-                scaled = ahead.tile([P, UNIT], F32, name="scaled")
+                n = FIRST_UNIT[level] + u
                 nc.vector.tensor_scalar(
-                    scaled[:], scores[:], -SCALE, None, op0=ALU.mult, op1=ALU.min, accum_out=lowest_of[b][:, n : n + 1]
+                    scaled[:, j * UNIT : (j + 1) * UNIT],
+                    scores[:],
+                    -SCALE,
+                    None,
+                    op0=ALU.mult,
+                    op1=ALU.min,
+                    accum_out=lowest_of[b][:, n : n + 1],
                 )
-                scaled_of[state].append(scaled)
-            nc.vector.tensor_reduce(
-                shifts_of[b][:, slot : slot + 1], lowest_of[b][:, 0 : (slot + 1) * STATE_UNITS], axis=AXIS.X, op=ALU.min
-            )
+            scaled_of[piece] = scaled
+            if closes_state(piece):
+                settle(piece)
+
+        def settle(piece):
+            b, level, c = piece
+            slot = slot_of[state_of(piece)]
+            seen = FIRST_UNIT[level] + (c + 1) * PIECE_UNITS
+            nc.vector.tensor_reduce(shifts_of[b][:, slot : slot + 1], lowest_of[b][:, 0:seen], axis=AXIS.X, op=ALU.min)
             if slot > 0:
                 nc.scalar.activation(
                     decays_of[b][:, slot : slot + 1],
@@ -112,53 +140,57 @@ def tile_cascadeattention_b_kernel(tc, qT, kpool, v0, k1, v1, k2, v2, offs, out)
                     scale=-1.0,
                 )
 
-        def weigh(state):
-            b, level, c = state
-            slot = slot_of[state]
-            weights = rows.tile([P, STATE], BF16, name="weights")
-            for j in range(STATE_UNITS):
-                nc.scalar.activation(
-                    weights[:, j * UNIT : (j + 1) * UNIT],
-                    scaled_of[state][j][:],
-                    EXP,
-                    bias=shifts_of[b][:, slot : slot + 1],
-                    scale=-1.0,
-                )
+        def weigh(piece):
+            b, level, c = piece
+            slot = slot_of[state_of(piece)]
+            weights = rows.tile([P, PIECE], BF16, name="weights")
+            nc.scalar.activation(
+                weights[:], scaled_of[piece][:], EXP, bias=shifts_of[b][:, slot : slot + 1], scale=-1.0
+            )
             words = weights[:].bitcast(F32)
             flipped_bank = flip_banks.tile([P, GROUPS * P], F32, name="flipped_bank")
             for k in range(GROUPS):
                 nc.tensor.transpose(flipped_bank[:, k * P : (k + 1) * P], words[:, k * P : (k + 1) * P], identity[:])
             if level == 0:
-                flipped = held.tile([P, STATE], BF16, name="flipped_%d_%d" % (b, c))
+                flipped = held.tile([P, PIECE], BF16, name="flipped_%d_%d" % (b, c))
             else:
-                flipped = columns.tile([P, STATE], BF16, name="flipped")
-            if level > 0 and slot % 2 == 0:
-                nc.scalar.copy(flipped[:], flipped_bank[:].bitcast(BF16))
-            else:
+                flipped = columns.tile([P, PIECE], BF16, name="flipped")
+            if order.index(piece) % 2 == 0:
                 nc.vector.tensor_copy(flipped[:], flipped_bank[:].bitcast(BF16))
-            flipped_of[state] = flipped
+            else:
+                nc.scalar.copy(flipped[:], flipped_bank[:].bitcast(BF16))
+            flipped_of[piece] = flipped
 
-        def combine(state):
-            b, level, c = state
-            slot = slot_of[state]
-            product = sum_banks.tile([P, D + 1], F32, name="product", tag="sum_bank")
-            halves = flipped_of[state]
+        def combine(piece):
+            b, level, c = piece
+            state = state_of(piece)
+            if opens_state(piece):
+                product_of[state] = sum_banks.tile([P, D + 1], F32, name="product", tag="sum_bank")
+            product = product_of[state]
             for k in range(GROUPS):
                 for r in range(PAIR):
                     nc.tensor.matmul(
                         product[:],
-                        halves[:, k * GROUP + r : (k + 1) * GROUP : PAIR],
+                        flipped_of[piece][:, k * GROUP + r : (k + 1) * GROUP : PAIR],
                         values_of[(b, level)][:, c * GROUPS + k, r, 0 : D + 1],
-                        start=(k == 0 and r == 0),
-                        stop=(k == GROUPS - 1 and r == PAIR - 1),
+                        start=(opens_state(piece) and k == 0 and r == 0),
+                        stop=(closes_state(piece) and k == GROUPS - 1 and r == PAIR - 1),
                     )
+            if closes_state(piece):
+                merge(state)
+
+        def merge(state):
+            b = state[0]
+            slot = slot_of[state]
             total = total_of[b]
             if slot == 0:
-                nc.vector.tensor_copy(total[:], product[:])
+                nc.vector.tensor_copy(total[:], product_of[state][:])
             else:
                 nc.vector.scalar_tensor_tensor(
-                    total[:], total[:], decays_of[b][:, slot : slot + 1], product[:], op0=ALU.mult, op1=ALU.add
+                    total[:], total[:], decays_of[b][:, slot : slot + 1], product_of[state][:], op0=ALU.mult, op1=ALU.add
                 )
+            if slot == states - 1:
+                finish(b)
 
         def finish(b):
             inverse = small.tile([P, 1], F32, name="inverse")
@@ -167,17 +199,15 @@ def tile_cascadeattention_b_kernel(tc, qT, kpool, v0, k1, v1, k2, v2, offs, out)
             nc.vector.tensor_scalar(result[:], total_of[b][:, 0:D], inverse[:], None, op0=ALU.mult)
             nc.sync.dma_start(out[b * H : (b + 1) * H, :], result[:])
 
-        for step in range(len(order) + 3):
+        for step in range(len(order) + COMBINE_LAG):
             if step < len(order):
                 score(order[step])
-            if 2 <= step < len(order) + 2:
-                weigh(order[step - 2])
-            if step - 3 >= len(shared):
-                state = order[step - 3]
-                waiting = [other for other in shared if other[0] == state[0]]
-                if slot_of[state] == len(waiting):
-                    for other in waiting:
-                        combine(other)
-                combine(state)
-                if slot_of[state] == STATES - 1:
-                    finish(state[0])
+            if 0 <= step - WEIGH_LAG < len(order):
+                weigh(order[step - WEIGH_LAG])
+            if step - COMBINE_LAG >= len(shared):
+                piece = order[step - COMBINE_LAG]
+                if piece[1] == 1 and piece[2] == 0:
+                    for other in shared:
+                        if other[0] == piece[0]:
+                            combine(other)
+                combine(piece)

@@ -16,7 +16,6 @@ PIECE_UNITS = 2
 PIECE = PIECE_UNITS * UNIT
 STATE_PIECES = 2
 LENGTH = (N, L1, L2)
-FIRST_UNIT = (0, N // UNIT, (N + L1) // UNIT)
 UNITS = (N + L1 + L2) // UNIT
 PAIR = 2
 GROUP = PAIR * P
@@ -34,8 +33,8 @@ def tile_cascadeattention_b_kernel(tc, qT, kpool, v0, k1, v1, k2, v2, offs, out)
     with (
         tc.tile_pool(name="held", bufs=1) as held,
         tc.tile_pool(name="small", bufs=4) as small,
-        tc.tile_pool(name="ahead", bufs=10) as ahead,
-        tc.tile_pool(name="rows", bufs=4) as rows,
+        tc.tile_pool(name="ahead", bufs=5) as ahead,
+        tc.tile_pool(name="rows", bufs=3) as rows,
         tc.tile_pool(name="columns", bufs=12) as columns,
         tc.psum_pool(name="score_banks", bufs=3) as score_banks,
         tc.psum_pool(name="flip_banks", bufs=3) as flip_banks,
@@ -43,7 +42,12 @@ def tile_cascadeattention_b_kernel(tc, qT, kpool, v0, k1, v1, k2, v2, offs, out)
     ):
         shared = [(b, 0, c) for b in range(B) for c in range(LENGTH[0] // PIECE)]
         private = [(b, level, c) for b in range(B) for level in (1, 2) for c in range(LENGTH[level] // PIECE)]
-        order = shared + private
+        early = private[:STATE_PIECES]
+        deferred = early + shared
+        order = deferred + private[STATE_PIECES:]
+        rank_of = {}
+        for piece in order:
+            rank_of[piece] = len([other for other in rank_of if other[0] == piece[0]])
 
         def state_of(piece):
             b, level, c = piece
@@ -51,6 +55,10 @@ def tile_cascadeattention_b_kernel(tc, qT, kpool, v0, k1, v1, k2, v2, offs, out)
 
         def opens_state(piece):
             return piece[2] % STATE_PIECES == 0
+
+        def keys_in(state):
+            b, level, s = state
+            return min(STATE_PIECES * PIECE, LENGTH[level] - s * STATE_PIECES * PIECE)
 
         def closes_state(piece):
             b, level, c = piece
@@ -76,6 +84,8 @@ def tile_cascadeattention_b_kernel(tc, qT, kpool, v0, k1, v1, k2, v2, offs, out)
             return values
 
         queries = load_keys("queries", qT)
+        first_keys = held.tile([D, L1], BF16, name="keys_0_1")
+        nc.sync.dma_start(first_keys[:, 0 : len(early) * PIECE], k1[0][:, 0 : len(early) * PIECE])
         offsets = held.tile([P, N // 16], U16, name="offsets")
         nc.sync.dma_start(offsets[:], offs)
         key_pool = load_keys("key_pool", kpool)
@@ -85,7 +95,11 @@ def tile_cascadeattention_b_kernel(tc, qT, kpool, v0, k1, v1, k2, v2, offs, out)
         for b in range(B):
             values_of[(b, 0)] = shared_values
             for level, key_source, value_source in ((1, k1, v1), (2, k2, v2)):
-                keys_of[(b, level)] = load_keys("keys_%d_%d" % (b, level), key_source[b])
+                if (b, level) == (0, 1):
+                    nc.sync.dma_start(first_keys[:, len(early) * PIECE :], key_source[b][:, len(early) * PIECE :])
+                    keys_of[(b, level)] = first_keys
+                else:
+                    keys_of[(b, level)] = load_keys("keys_%d_%d" % (b, level), key_source[b])
                 values_of[(b, level)] = load_values("values_%d_%d" % (b, level), value_source[b])
         identity = held.tile([P, P], F32, name="identity")
         make_identity(nc, identity[:])
@@ -95,12 +109,16 @@ def tile_cascadeattention_b_kernel(tc, qT, kpool, v0, k1, v1, k2, v2, offs, out)
         decays_of = [held.tile([P, states], F32, name="decays_%d" % b) for b in range(B)]
         total_of = [held.tile([P, D + 1], F32, name="total_%d" % b) for b in range(B)]
         scaled_of = {}
+        weights_of = {}
         flipped_of = {}
         product_of = {}
 
         def score(piece):
             b, level, c = piece
-            scaled = ahead.tile([P, PIECE], F32, name="scaled")
+            state = state_of(piece)
+            if opens_state(piece):
+                scaled_of[state] = ahead.tile([P, keys_in(state)], F32, name="scaled")
+            scaled = scaled_of[state]
             for j in range(PIECE_UNITS):
                 u = c * PIECE_UNITS + j
                 if piece == shared[-1]:
@@ -112,9 +130,9 @@ def tile_cascadeattention_b_kernel(tc, qT, kpool, v0, k1, v1, k2, v2, offs, out)
                 else:
                     moving = keys_of[(b, level)][:, u * UNIT : (u + 1) * UNIT]
                 nc.tensor.matmul(scores[:], queries[:, b * H : (b + 1) * H], moving, start=True, stop=True)
-                n = FIRST_UNIT[level] + u
+                n = rank_of[piece] * PIECE_UNITS + j
                 nc.vector.tensor_scalar(
-                    scaled[:, j * UNIT : (j + 1) * UNIT],
+                    scaled[:, (u % (STATE_PIECES * PIECE_UNITS)) * UNIT : (u % (STATE_PIECES * PIECE_UNITS) + 1) * UNIT],
                     scores[:],
                     -SCALE,
                     None,
@@ -122,14 +140,13 @@ def tile_cascadeattention_b_kernel(tc, qT, kpool, v0, k1, v1, k2, v2, offs, out)
                     op1=ALU.min,
                     accum_out=lowest_of[b][:, n : n + 1],
                 )
-            scaled_of[piece] = scaled
             if closes_state(piece):
                 settle(piece)
 
         def settle(piece):
             b, level, c = piece
             slot = slot_of[state_of(piece)]
-            seen = FIRST_UNIT[level] + (c + 1) * PIECE_UNITS
+            seen = (rank_of[piece] + 1) * PIECE_UNITS
             nc.vector.tensor_reduce(shifts_of[b][:, slot : slot + 1], lowest_of[b][:, 0:seen], axis=AXIS.X, op=ALU.min)
             if slot > 0:
                 nc.scalar.activation(
@@ -142,17 +159,20 @@ def tile_cascadeattention_b_kernel(tc, qT, kpool, v0, k1, v1, k2, v2, offs, out)
 
         def weigh(piece):
             b, level, c = piece
-            slot = slot_of[state_of(piece)]
-            weights = rows.tile([P, PIECE], BF16, name="weights")
-            nc.scalar.activation(
-                weights[:], scaled_of[piece][:], EXP, bias=shifts_of[b][:, slot : slot + 1], scale=-1.0
-            )
-            words = weights[:].bitcast(F32)
+            state = state_of(piece)
+            slot = slot_of[state]
+            if opens_state(piece):
+                weights_of[state] = rows.tile([P, keys_in(state)], BF16, name="weights")
+                nc.scalar.activation(
+                    weights_of[state][:], scaled_of[state][:], EXP, bias=shifts_of[b][:, slot : slot + 1], scale=-1.0
+                )
+            words = weights_of[state][:].bitcast(F32)
             flipped_bank = flip_banks.tile([P, GROUPS * P], F32, name="flipped_bank")
             for k in range(GROUPS):
-                nc.tensor.transpose(flipped_bank[:, k * P : (k + 1) * P], words[:, k * P : (k + 1) * P], identity[:])
-            if level == 0:
-                flipped = held.tile([P, PIECE], BF16, name="flipped_%d_%d" % (b, c))
+                g = (c % STATE_PIECES) * GROUPS + k
+                nc.tensor.transpose(flipped_bank[:, k * P : (k + 1) * P], words[:, g * P : (g + 1) * P], identity[:])
+            if piece in deferred:
+                flipped = held.tile([P, PIECE], BF16, name="flipped_%d_%d_%d" % (b, level, c))
             else:
                 flipped = columns.tile([P, PIECE], BF16, name="flipped")
             if order.index(piece) % 2 == 0:
@@ -204,10 +224,10 @@ def tile_cascadeattention_b_kernel(tc, qT, kpool, v0, k1, v1, k2, v2, offs, out)
                 score(order[step])
             if 0 <= step - WEIGH_LAG < len(order):
                 weigh(order[step - WEIGH_LAG])
-            if step - COMBINE_LAG >= len(shared):
+            if step - COMBINE_LAG >= len(deferred):
                 piece = order[step - COMBINE_LAG]
-                if piece[1] == 1 and piece[2] == 0:
-                    for other in shared:
-                        if other[0] == piece[0]:
-                            combine(other)
+                waiting = [other for other in deferred if other[0] == piece[0]]
+                if rank_of[piece] == len(waiting):
+                    for other in waiting:
+                        combine(other)
                 combine(piece)

@@ -176,9 +176,9 @@ def tile_cascadeattention_b_kernel(tc, qT, kpool, v0, k1, v1, k2, v2, offs, out)
             else:
                 flipped = columns.tile([P, PIECE], BF16, name="flipped")
             if order.index(piece) % 2 == 0:
-                nc.vector.tensor_copy(flipped[:], flipped_bank[:].bitcast(BF16))
+                nc.vector.tensor_copy(flipped[:].bitcast(F32), flipped_bank[:])
             else:
-                nc.scalar.copy(flipped[:], flipped_bank[:].bitcast(BF16))
+                nc.scalar.copy(flipped[:].bitcast(F32), flipped_bank[:])
             flipped_of[piece] = flipped
 
         def combine(piece):

@@ -175,7 +175,7 @@ def tile_cascadeattention_b_kernel(tc, qT, kpool, v0, k1, v1, k2, v2, offs, out)
                 flipped = held.tile([P, PIECE], BF16, name="flipped_%d_%d_%d" % (b, level, c))
             else:
                 flipped = columns.tile([P, PIECE], BF16, name="flipped")
-            if order.index(piece) % 2 == 0:
+            if order.index(piece) % 3 == 0:
                 nc.vector.tensor_copy(flipped[:].bitcast(F32), flipped_bank[:])
             else:
                 nc.scalar.copy(flipped[:].bitcast(F32), flipped_bank[:])

@@ -90,17 +90,15 @@ def tile_cascadeattention_b_kernel(tc, qT, kpool, v0, k1, v1, k2, v2, offs, out)
         nc.sync.dma_start(offsets[:], offs)
         key_pool = load_keys("key_pool", kpool)
         shared_values = load_values("shared_values", v0)
-        keys_of = {}
+        nc.sync.dma_start(first_keys[:, len(early) * PIECE :], k1[0][:, len(early) * PIECE :])
+        keys_of = {(0, 1): first_keys, (0, 2): load_keys("keys_0_2", k2[0])}
         values_of = {}
         for b in range(B):
             values_of[(b, 0)] = shared_values
             for level, key_source, value_source in ((1, k1, v1), (2, k2, v2)):
-                if (b, level) == (0, 1):
-                    nc.sync.dma_start(first_keys[:, len(early) * PIECE :], key_source[b][:, len(early) * PIECE :])
-                    keys_of[(b, level)] = first_keys
-                else:
-                    keys_of[(b, level)] = load_keys("keys_%d_%d" % (b, level), key_source[b])
                 values_of[(b, level)] = load_values("values_%d_%d" % (b, level), value_source[b])
+                if b + 1 < B:
+                    keys_of[(b + 1, level)] = load_keys("keys_%d_%d" % (b + 1, level), key_source[b + 1])
         identity = held.tile([P, P], F32, name="identity")
         make_identity(nc, identity[:])
 

@@ -22,8 +22,8 @@ GROUP = PAIR * P
 GROUPS = PIECE // GROUP
 ROW = D + 16
 
-WEIGH_LAG = 4
-COMBINE_LAG = 7
+WEIGH_LAG = 5
+COMBINE_LAG = 8
 
 FLOPS = 4 * M * (N + L1 + L2) * D
 

import concourse.mybir as mybir
from concourse.masks import make_identity

BF16 = mybir.dt.bfloat16
F32 = mybir.dt.float32
U16 = mybir.dt.uint16
EXP = mybir.ActivationFunctionType.Exp
ALU = mybir.AluOpType
AXIS = mybir.AxisListType

P = 128
D, N, B, H, M, L1, L2 = 128, 2048, 4, 128, 512, 4096, 3072
SCALE = D**-0.5
UNIT = 512
PIECE_UNITS = 2
PIECE = PIECE_UNITS * UNIT
STATE_PIECES = 2
LENGTH = (N, L1, L2)
UNITS = (N + L1 + L2) // UNIT
PAIR = 2
GROUP = PAIR * P
GROUPS = PIECE // GROUP
ROW = D + 16

WEIGH_LAG = 5
COMBINE_LAG = 8

FLOPS = 4 * M * (N + L1 + L2) * D


def tile_cascadeattention_b_kernel(tc, qT, kpool, v0, k1, v1, k2, v2, offs, out):
    nc = tc.nc
    with (
        tc.tile_pool(name="held", bufs=1) as held,
        tc.tile_pool(name="small", bufs=4) as small,
        tc.tile_pool(name="ahead", bufs=5) as ahead,
        tc.tile_pool(name="rows", bufs=3) as rows,
        tc.tile_pool(name="columns", bufs=12) as columns,
        tc.psum_pool(name="score_banks", bufs=3) as score_banks,
        tc.psum_pool(name="flip_banks", bufs=3) as flip_banks,
        tc.psum_pool(name="sum_banks", bufs=2) as sum_banks,
    ):
        shared = [(b, 0, c) for b in range(B) for c in range(LENGTH[0] // PIECE)]
        private = [(b, level, c) for b in range(B) for level in (1, 2) for c in range(LENGTH[level] // PIECE)]
        early = private[:STATE_PIECES]
        deferred = early + shared
        order = deferred + private[STATE_PIECES:]
        rank_of = {}
        for piece in order:
            rank_of[piece] = len([other for other in rank_of if other[0] == piece[0]])

        def state_of(piece):
            b, level, c = piece
            return (b, level, c // STATE_PIECES)

        def opens_state(piece):
            return piece[2] % STATE_PIECES == 0

        def keys_in(state):
            b, level, s = state
            return min(STATE_PIECES * PIECE, LENGTH[level] - s * STATE_PIECES * PIECE)

        def closes_state(piece):
            b, level, c = piece
            return c % STATE_PIECES == STATE_PIECES - 1 or c == LENGTH[level] // PIECE - 1

        slot_of = {}
        for piece in order:
            if opens_state(piece):
                slot_of[state_of(piece)] = len([other for other in slot_of if other[0] == piece[0]])
        states = len([state for state in slot_of if state[0] == 0])

        def load_keys(name, source):
            keys = held.tile([D, source.shape[1]], BF16, name=name)
            nc.sync.dma_start(keys[:], source)
            return keys

        def load_values(name, source):
            values = held.tile([P, source.shape[0] // GROUP, PAIR, ROW], BF16, name=name)
            nc.gpsimd.memset(values[:, :, :, D:ROW], 1.0)
            by_parity = source.rearrange("(g p r) d -> p g r d", p=P, r=PAIR)
            for r in range(PAIR):
                nc.sync.dma_start(values[:, :, r, 0:D], by_parity[:, :, r, :])
            return values

        queries = load_keys("queries", qT)
        first_keys = held.tile([D, L1], BF16, name="keys_0_1")
        nc.sync.dma_start(first_keys[:, 0 : len(early) * PIECE], k1[0][:, 0 : len(early) * PIECE])
        offsets = held.tile([P, N // 16], U16, name="offsets")
        nc.sync.dma_start(offsets[:], offs)
        key_pool = load_keys("key_pool", kpool)
        shared_values = load_values("shared_values", v0)
        nc.sync.dma_start(first_keys[:, len(early) * PIECE :], k1[0][:, len(early) * PIECE :])
        keys_of = {(0, 1): first_keys, (0, 2): load_keys("keys_0_2", k2[0])}
        values_of = {}
        for b in range(B):
            values_of[(b, 0)] = shared_values
            for level, key_source, value_source in ((1, k1, v1), (2, k2, v2)):
                values_of[(b, level)] = load_values("values_%d_%d" % (b, level), value_source[b])
                if b + 1 < B:
                    keys_of[(b + 1, level)] = load_keys("keys_%d_%d" % (b + 1, level), key_source[b + 1])
        identity = held.tile([P, P], F32, name="identity")
        make_identity(nc, identity[:])

        lowest_of = [held.tile([P, UNITS], F32, name="lowest_%d" % b) for b in range(B)]
        shifts_of = [held.tile([P, states], F32, name="shifts_%d" % b) for b in range(B)]
        decays_of = [held.tile([P, states], F32, name="decays_%d" % b) for b in range(B)]
        total_of = [held.tile([P, D + 1], F32, name="total_%d" % b) for b in range(B)]
        scaled_of = {}
        weights_of = {}
        flipped_of = {}
        product_of = {}

        def score(piece):
            b, level, c = piece
            state = state_of(piece)
            if opens_state(piece):
                scaled_of[state] = ahead.tile([P, keys_in(state)], F32, name="scaled")
            scaled = scaled_of[state]
            for j in range(PIECE_UNITS):
                u = c * PIECE_UNITS + j
                if piece == shared[-1]:
                    scores = sum_banks.tile([P, UNIT], F32, name="scores", tag="sum_bank")
                else:
                    scores = score_banks.tile([P, UNIT], F32, name="scores")
                if level == 0:
                    moving = key_pool[:].indirect(offsets[:, u * UNIT // 16 : (u + 1) * UNIT // 16])
                else:
                    moving = keys_of[(b, level)][:, u * UNIT : (u + 1) * UNIT]
                nc.tensor.matmul(scores[:], queries[:, b * H : (b + 1) * H], moving, start=True, stop=True)
                n = rank_of[piece] * PIECE_UNITS + j
                nc.vector.tensor_scalar(
                    scaled[:, (u % (STATE_PIECES * PIECE_UNITS)) * UNIT : (u % (STATE_PIECES * PIECE_UNITS) + 1) * UNIT],
                    scores[:],
                    -SCALE,
                    None,
                    op0=ALU.mult,
                    op1=ALU.min,
                    accum_out=lowest_of[b][:, n : n + 1],
                )
            if closes_state(piece):
                settle(piece)

        def settle(piece):
            b, level, c = piece
            slot = slot_of[state_of(piece)]
            seen = (rank_of[piece] + 1) * PIECE_UNITS
            nc.vector.tensor_reduce(shifts_of[b][:, slot : slot + 1], lowest_of[b][:, 0:seen], axis=AXIS.X, op=ALU.min)
            if slot > 0:
                nc.scalar.activation(
                    decays_of[b][:, slot : slot + 1],
                    shifts_of[b][:, slot - 1 : slot],
                    EXP,
                    bias=shifts_of[b][:, slot : slot + 1],
                    scale=-1.0,
                )

        def weigh(piece):
            b, level, c = piece
            state = state_of(piece)
            slot = slot_of[state]
            if opens_state(piece):
                weights_of[state] = rows.tile([P, keys_in(state)], BF16, name="weights")
                nc.scalar.activation(
                    weights_of[state][:], scaled_of[state][:], EXP, bias=shifts_of[b][:, slot : slot + 1], scale=-1.0
                )
            words = weights_of[state][:].bitcast(F32)
            flipped_bank = flip_banks.tile([P, GROUPS * P], F32, name="flipped_bank")
            for k in range(GROUPS):
                g = (c % STATE_PIECES) * GROUPS + k
                nc.tensor.transpose(flipped_bank[:, k * P : (k + 1) * P], words[:, g * P : (g + 1) * P], identity[:])
            if piece in deferred:
                flipped = held.tile([P, PIECE], BF16, name="flipped_%d_%d_%d" % (b, level, c))
            else:
                flipped = columns.tile([P, PIECE], BF16, name="flipped")
            if order.index(piece) % 3 == 0:
                nc.vector.tensor_copy(flipped[:].bitcast(F32), flipped_bank[:])
            else:
                nc.scalar.copy(flipped[:].bitcast(F32), flipped_bank[:])
            flipped_of[piece] = flipped

        def combine(piece):
            b, level, c = piece
            state = state_of(piece)
            if opens_state(piece):
                product_of[state] = sum_banks.tile([P, D + 1], F32, name="product", tag="sum_bank")
            product = product_of[state]
            for k in range(GROUPS):
                for r in range(PAIR):
                    nc.tensor.matmul(
                        product[:],
                        flipped_of[piece][:, k * GROUP + r : (k + 1) * GROUP : PAIR],
                        values_of[(b, level)][:, c * GROUPS + k, r, 0 : D + 1],
                        start=(opens_state(piece) and k == 0 and r == 0),
                        stop=(closes_state(piece) and k == GROUPS - 1 and r == PAIR - 1),
                    )
            if closes_state(piece):
                merge(state)

        def merge(state):
            b = state[0]
            slot = slot_of[state]
            total = total_of[b]
            if slot == 0:
                nc.vector.tensor_copy(total[:], product_of[state][:])
            else:
                nc.vector.scalar_tensor_tensor(
                    total[:], total[:], decays_of[b][:, slot : slot + 1], product_of[state][:], op0=ALU.mult, op1=ALU.add
                )
            if slot == states - 1:
                finish(b)

        def finish(b):
            inverse = small.tile([P, 1], F32, name="inverse")
            nc.vector.reciprocal(inverse[:], total_of[b][:, D : D + 1])
            result = small.tile([P, D], F32, name="result")
            nc.vector.tensor_scalar(result[:], total_of[b][:, 0:D], inverse[:], None, op0=ALU.mult)
            nc.sync.dma_start(out[b * H : (b + 1) * H, :], result[:])

        for step in range(len(order) + COMBINE_LAG):
            if step < len(order):
                score(order[step])
            if 0 <= step - WEIGH_LAG < len(order):
                weigh(order[step - WEIGH_LAG])
            if step - COMBINE_LAG >= len(deferred):
                piece = order[step - COMBINE_LAG]
                waiting = [other for other in deferred if other[0] == piece[0]]
                if rank_of[piece] == len(waiting):
                    for other in waiting:
                        combine(other)
                combine(piece)
